import numpy as np
import ml_dtypes


def mxq(x, axis, fmt="e4m3"):
    dtype, down = {"e4m3": (ml_dtypes.float8_e4m3fn, 7), "e5m2": (ml_dtypes.float8_e5m2, 14)}[fmt]
    v = np.moveaxis(np.asarray(x, np.float32).astype(ml_dtypes.bfloat16).astype(np.float64), axis, -1)
    blocks = v.reshape(v.shape[:-1] + (-1, 32))
    amax = np.abs(blocks).max(-1, keepdims=True)
    byte = np.maximum(np.where(amax > 0, np.frexp(amax)[1] - 1 + 127, 0) - down, 1)
    scale = np.exp2(byte - 127.0)
    codes = (blocks / scale).astype(np.float32).astype(dtype).astype(np.float64)
    return np.moveaxis((codes * scale).reshape(v.shape), -1, axis)


WIDE = False


def mx_kscale(k):
    if not WIDE:
        return np.ones(k)
    levels = np.array([10, -10, 5, -5, 0])
    a = np.random.permutation(np.resize(levels, k // 512 * 4)).reshape(k // 512, 4)
    idx = np.arange(k)
    return np.exp2(a[idx // 512, idx % 128 // 32])


BF16 = ml_dtypes.bfloat16


def bf(x):
    return np.asarray(x, np.float32).astype(BF16)


def f64(x):
    return np.asarray(x).astype(np.float64)


BQ, BK, L, H, DH = 64, 4, 128, 4, 128
D = H * DH


def setup_inputs():
    s, t = mx_kscale(D), mx_kscale(D)
    amp_q = 0.5 + np.random.random((BQ, 1, 1))
    amp_k = 0.5 + np.random.random((BK, 1, 1))
    return {
        "query_states": bf(np.random.standard_normal((BQ, L, D)) * amp_q * s),
        "key_states": bf(np.random.standard_normal((BK, L, D)) * amp_k * s),
        "Wq": bf(np.random.standard_normal((D, D)) * 0.8 / np.sqrt(D) * t[:, None] / s[None, :]),
        "bq": bf(np.random.standard_normal(D) * 0.3 * t),
        "Wk": bf(np.random.standard_normal((D, D)) * 0.8 / np.sqrt(D) / t[:, None] / s[None, :]),
        "bk": bf(np.random.standard_normal(D) * 0.3 / t),
        "logit_scale": bf(-1.5 + 0.1 * np.random.standard_normal(1)),
    }


def reference(query_states, key_states, Wq, bq, Wk, bk, logit_scale):
    q = (mxq(f64(query_states).reshape(BQ * L, D), 1, "e4m3") @ mxq(f64(Wq), 1, "e4m3").T) + f64(bq)
    k = (mxq(f64(key_states).reshape(BK * L, D), 1, "e4m3") @ mxq(f64(Wk), 1, "e4m3").T) + f64(bk)
    retrieve = mxq(q, 1, "e4m3") @ mxq(k, 1, "e4m3").T
    retrieve = retrieve.reshape(BQ, L, BK, L).transpose(0, 2, 1, 3)
    t2v = retrieve.max(axis=-1).sum(axis=2) / L
    v2t = retrieve.max(axis=-2).sum(axis=2) / L
    return np.exp(f64(logit_scale)) * (t2v + v2t) / 2.0

@@ -1,0 +1,183 @@
+from contextlib import ExitStack
+
+import concourse.mybir as mybir
+from concourse.masks import make_identity
+
+F32 = mybir.dt.float32
+BF16 = mybir.dt.bfloat16
+U32 = mybir.dt.uint32
+U8 = mybir.dt.uint8
+FP8X4 = mybir.dt.float8_e4m3fn_x4
+ALU = mybir.AluOpType
+ACT = mybir.ActivationFunctionType
+AXIS_X = mybir.AxisListType.X
+
+P = 128
+PACK = 4
+BQ, BK, L, D = 64, 4, 128, 512
+GROUP = 4
+ROWS = GROUP * L
+N_GROUPS = BQ // GROUP
+WORDS = D // 2
+
+FLOPS = 2 * D * D * (BQ + BK) * L + 2 * (BQ * L) * (BK * L) * D
+
+
+def tile_attention_pa_t_kernel(tc, query_states, key_states, Wq, bq, Wk, bk, logit_scale, out):
+    nc = tc.nc
+    with ExitStack() as stack:
+        const = stack.enter_context(tc.tile_pool(name="const", bufs=1))
+        xpool = stack.enter_context(tc.tile_pool(name="xpool", bufs=N_GROUPS))
+        stage = stack.enter_context(tc.tile_pool(name="stage", bufs=3))
+        psum = stack.enter_context(tc.psum_pool(name="psum", bufs=2))
+
+        wk_raw = const.tile([P, GROUP * D], BF16, name="wk_raw")
+        ks_raw = const.tile([P, GROUP * D], BF16, name="ks_raw")
+        wq_raw = const.tile([P, GROUP * D], BF16, name="wq_raw")
+        nc.sync.dma_start(out=wk_raw, in_=Wk.rearrange("(m t) d -> m (t d)", t=PACK))
+        nc.sync.dma_start(
+            out=ks_raw.rearrange("p (s d) -> p s d", s=GROUP), in_=key_states.rearrange("s l d -> l s d")
+        )
+        nc.sync.dma_start(out=wq_raw, in_=Wq.rearrange("(m t) d -> m (t d)", t=PACK))
+        x_raw = []
+        for g in range(N_GROUPS):
+            xg = xpool.tile([P, GROUP * D], BF16, name="x_raw", tag="x_raw")
+            nc.sync.dma_start(
+                out=xg.rearrange("p (s d) -> p s d", s=GROUP),
+                in_=query_states[g * GROUP : (g + 1) * GROUP].rearrange("s l d -> l s d"),
+            )
+            x_raw.append(xg)
+
+        bk_bf = const.tile([P, PACK], BF16, name="bk_bf")
+        bq_bf = const.tile([P, PACK], BF16, name="bq_bf")
+        ls_bf = const.tile([P, 1], BF16, name="ls_bf")
+        nc.scalar.dma_start(out=bk_bf, in_=bk.rearrange("(p t) -> p t", t=PACK))
+        nc.scalar.dma_start(out=bq_bf, in_=bq.rearrange("(p t) -> p t", t=PACK))
+        nc.scalar.dma_start(out=ls_bf, in_=logit_scale.partition_broadcast(P))
+
+        ident = const.tile([P, P], F32, name="ident")
+        make_identity(nc, ident)
+        ones = const.tile([P, P], F32, name="ones")
+        nc.gpsimd.memset(ones, 1.0)
+        gain = const.tile([P, 1], F32, name="gain")
+        nc.scalar.activation(out=gain, in_=ls_bf, func=ACT.Exp)
+        bk_f = const.tile([P, PACK], F32, name="bk_f")
+        bq_f = const.tile([P, PACK], F32, name="bq_f")
+        nc.vector.tensor_copy(out=bk_f, in_=bk_bf)
+        nc.vector.tensor_copy(out=bq_f, in_=bq_bf)
+
+        def quantise_rows(raw, codes, scales):
+            raw_words = raw.bitcast(F32)
+            grouped = stage.tile([P, ROWS * PACK], BF16, name="grouped_in", tag="grouped_in", align_bytes=64)
+            grouped_words = grouped.bitcast(F32).rearrange("p (s r u) -> p s r u", s=GROUP, u=2)
+            for half in range(2):
+                bank = psum.tile([P, 2, 2, P], F32, name="xt", tag="xt")
+                for s in range(2):
+                    for u in range(2):
+                        first = (2 * half + s) * WORDS + u * P
+                        nc.tensor.transpose(bank[:, s, u, :], raw_words[:, first : first + P], ident)
+                nc.scalar.copy(
+                    out=grouped_words[:, 2 * half : 2 * half + 2], in_=bank.rearrange("p s u r -> p s r u")
+                )
+            nc.vector.quantize_mx(out=codes.bitcast(FP8X4), scales=scales, in_=grouped)
+
+        def project(w_codes, w_scales, in_codes, in_scales, bias, codes, scales, tag, bufs):
+            planar = stage.tile([P, PACK, ROWS], BF16, name="planar", tag="planar")
+            for t in range(PACK):
+                acc = psum.tile([P, ROWS], F32, name="acc", tag=tag, bufs=bufs)
+                nc.tensor.matmul_mx(
+                    out=acc,
+                    lhsT=w_codes[:, t * P : (t + 1) * P].bitcast(FP8X4),
+                    lhsT_scale=w_scales[:, t * P : (t + 1) * P],
+                    rhs=in_codes.bitcast(FP8X4),
+                    rhs_scale=in_scales,
+                    start=True,
+                    stop=True,
+                )
+                nc.scalar.activation(out=planar[:, t, :], in_=acc, func=ACT.Identity, bias=bias[:, t : t + 1], scale=1.0)
+            grouped = stage.tile([P, ROWS * PACK], BF16, name="grouped_out", tag="grouped_out", align_bytes=64)
+            nc.scalar.copy(
+                out=grouped.rearrange("p (c i t) -> p c t i", i=4, t=PACK),
+                in_=planar.rearrange("p t (c i) -> p c t i", i=4),
+            )
+            nc.vector.quantize_mx(out=codes.bitcast(FP8X4), scales=scales, in_=grouped)
+
+        def mx_tiles(pool, name):
+            codes = pool.tile([P, ROWS], U32, name=name + "_codes", tag=name + "_codes", align_bytes=64)
+            scales = pool.tile([P, ROWS], U8, name=name + "_scales", tag=name + "_scales", align_bytes=64)
+            return codes, scales
+
+        wk_codes, wk_scales = mx_tiles(const, "wk")
+        ks_codes, ks_scales = mx_tiles(const, "ks")
+        wq_codes, wq_scales = mx_tiles(const, "wq")
+        k_codes, k_scales = mx_tiles(const, "k")
+        quantise_rows(wk_raw, wk_codes, wk_scales)
+        quantise_rows(ks_raw, ks_codes, ks_scales)
+        quantise_rows(wq_raw, wq_codes, wq_scales)
+        project(wk_codes, wk_scales, ks_codes, ks_scales, bk_f, k_codes, k_scales, "r", 4)
+
+        row_max = const.tile([P, BQ, BK], F32, name="row_max")
+        col_max = const.tile([P, BK, BQ], F32, name="col_max")
+
+        x_mx = {}
+        q_mx = {}
+
+        def stage_a(g):
+            x_mx[g] = mx_tiles(stage, "x")
+            quantise_rows(x_raw[g], x_mx[g][0], x_mx[g][1])
+
+        def stage_b(g):
+            q_mx[g] = mx_tiles(stage, "q")
+            project(wq_codes, wq_scales, x_mx[g][0], x_mx[g][1], bq_f, q_mx[g][0], q_mx[g][1], "proj", 2)
+
+        def stage_c(g):
+            q_codes, q_scales = q_mx[g]
+            for s in range(GROUP):
+                r = psum.tile([P, BK * L], F32, name="r", tag="r", bufs=4)
+                nc.tensor.matmul_mx(
+                    out=r,
+                    lhsT=q_codes[:, s * L : (s + 1) * L].bitcast(FP8X4),
+                    lhsT_scale=q_scales[:, s * L : (s + 1) * L],
+                    rhs=k_codes.bitcast(FP8X4),
+                    rhs_scale=k_scales,
+                    start=True,
+                    stop=True,
+                )
+                nc.vector.tensor_reduce(
+                    out=row_max[:, g * GROUP + s, :], in_=r.rearrange("p (b m) -> p b m", b=BK), axis=AXIS_X, op=ALU.max
+                )
+            for b in range(BK):
+                rt = psum.tile([P, ROWS], F32, name="rt", tag="r", bufs=4)
+                nc.tensor.matmul_mx(
+                    out=rt,
+                    lhsT=k_codes[:, b * L : (b + 1) * L].bitcast(FP8X4),
+                    lhsT_scale=k_scales[:, b * L : (b + 1) * L],
+                    rhs=q_codes.bitcast(FP8X4),
+                    rhs_scale=q_scales,
+                    start=True,
+                    stop=True,
+                )
+                nc.vector.tensor_reduce(
+                    out=col_max[:, b, g * GROUP : (g + 1) * GROUP],
+                    in_=rt.rearrange("p (a l) -> p a l", a=GROUP),
+                    axis=AXIS_X,
+                    op=ALU.max,
+                )
+
+        for step in range(N_GROUPS + 2):
+            if step < N_GROUPS:
+                stage_a(step)
+            if 1 <= step <= N_GROUPS:
+                stage_b(step - 1)
+            if step >= 2:
+                stage_c(step - 2)
+
+        both = const.tile([P, BQ, BK], F32, name="both")
+        nc.vector.tensor_tensor(out=both, in0=row_max, in1=col_max.rearrange("p b a -> p a b"), op=ALU.add)
+        sums = psum.tile([P, BQ * BK], F32, name="sums", tag="r", bufs=4)
+        nc.tensor.matmul(out=sums, lhsT=ones, rhs=both.rearrange("p a b -> p (a b)"), start=True, stop=True)
+        result = const.tile([P, BQ * BK], F32, name="result")
+        nc.vector.tensor_scalar(
+            out=result, in0=sums, scalar1=gain[:, 0:1], scalar2=1.0 / (2 * L), op0=ALU.mult, op1=ALU.mult
+        )
+        nc.sync.dma_start(out=out.rearrange("(o a) b -> o (a b)", o=1), in_=result[0:1, :])

@@ -19,6 +19,8 @@ GROUP = 4
 ROWS = GROUP * L
 N_GROUPS = BQ // GROUP
 WORDS = D // 2
+BANKS = 2 * GROUP
+GPSIMD_SAMPLES = 2
 
 FLOPS = 2 * D * D * (BQ + BK) * L + 2 * (BQ * L) * (BK * L) * D
 
@@ -30,6 +32,7 @@ def tile_attention_pa_t_kernel(tc, query_states, key_states, Wq, bq, Wk, bk, log
         xpool = stack.enter_context(tc.tile_pool(name="xpool", bufs=N_GROUPS))
         stage = stack.enter_context(tc.tile_pool(name="stage", bufs=3))
         psum = stack.enter_context(tc.psum_pool(name="psum", bufs=2))
+        stack.enter_context(tc.manual_schedule())
 
         wk_raw = const.tile([P, GROUP * D], BF16, name="wk_raw")
         ks_raw = const.tile([P, GROUP * D], BF16, name="ks_raw")
@@ -66,7 +69,15 @@ def tile_attention_pa_t_kernel(tc, query_states, key_states, Wq, bq, Wk, bk, log
         nc.vector.tensor_copy(out=bk_f, in_=bk_bf)
         nc.vector.tensor_copy(out=bq_f, in_=bq_bf)
 
-        def quantise_rows(raw, codes, scales):
+        def mx_tiles(pool, name):
+            codes = pool.tile([P, ROWS], U32, name=name + "_codes", tag=name + "_codes", align_bytes=64)
+            scales = pool.tile([P, ROWS], U8, name=name + "_scales", tag=name + "_scales", align_bytes=64)
+            return codes, scales
+
+        def quantise(grouped, operand):
+            nc.vector.quantize_mx(out=operand[0].bitcast(FP8X4), scales=operand[1], in_=grouped)
+
+        def features_to_partitions(raw, copies):
             raw_words = raw.bitcast(F32)
             grouped = stage.tile([P, ROWS * PACK], BF16, name="grouped_in", tag="grouped_in", align_bytes=64)
             grouped_words = grouped.bitcast(F32).rearrange("p (s r u) -> p s r u", s=GROUP, u=2)
@@ -76,106 +87,174 @@ def tile_attention_pa_t_kernel(tc, query_states, key_states, Wq, bq, Wk, bk, log
                     for u in range(2):
                         first = (2 * half + s) * WORDS + u * P
                         nc.tensor.transpose(bank[:, s, u, :], raw_words[:, first : first + P], ident)
-                nc.scalar.copy(
-                    out=grouped_words[:, 2 * half : 2 * half + 2], in_=bank.rearrange("p s u r -> p s r u")
-                )
-            nc.vector.quantize_mx(out=codes.bitcast(FP8X4), scales=scales, in_=grouped)
+                copies[half](out=grouped_words[:, 2 * half : 2 * half + 2], in_=bank.rearrange("p s u r -> p s r u"))
+            return grouped
 
-        def project(w_codes, w_scales, in_codes, in_scales, bias, codes, scales, tag, bufs):
-            planar = stage.tile([P, PACK, ROWS], BF16, name="planar", tag="planar")
-            for t in range(PACK):
-                acc = psum.tile([P, ROWS], F32, name="acc", tag=tag, bufs=bufs)
-                nc.tensor.matmul_mx(
-                    out=acc,
-                    lhsT=w_codes[:, t * P : (t + 1) * P].bitcast(FP8X4),
-                    lhsT_scale=w_scales[:, t * P : (t + 1) * P],
-                    rhs=in_codes.bitcast(FP8X4),
-                    rhs_scale=in_scales,
-                    start=True,
-                    stop=True,
-                )
-                nc.scalar.activation(out=planar[:, t, :], in_=acc, func=ACT.Identity, bias=bias[:, t : t + 1], scale=1.0)
-            grouped = stage.tile([P, ROWS * PACK], BF16, name="grouped_out", tag="grouped_out", align_bytes=64)
-            nc.scalar.copy(
-                out=grouped.rearrange("p (c i t) -> p c t i", i=4, t=PACK),
-                in_=planar.rearrange("p t (c i) -> p c t i", i=4),
+        def project_pass(weights, rows, t, tag, bufs):
+            acc = psum.tile([P, ROWS], F32, name="acc", tag=tag, bufs=bufs)
+            nc.tensor.matmul_mx(
+                out=acc,
+                lhsT=weights[0][:, t * P : (t + 1) * P].bitcast(FP8X4),
+                lhsT_scale=weights[1][:, t * P : (t + 1) * P],
+                rhs=rows[0].bitcast(FP8X4),
+                rhs_scale=rows[1],
+                start=True,
+                stop=True,
             )
-            nc.vector.quantize_mx(out=codes.bitcast(FP8X4), scales=scales, in_=grouped)
+            return acc
 
-        def mx_tiles(pool, name):
-            codes = pool.tile([P, ROWS], U32, name=name + "_codes", tag=name + "_codes", align_bytes=64)
-            scales = pool.tile([P, ROWS], U8, name=name + "_scales", tag=name + "_scales", align_bytes=64)
-            return codes, scales
+        def scalar_add_bias(dst, acc, bias):
+            nc.scalar.activation(out=dst, in_=acc, func=ACT.Identity, bias=bias, scale=1.0)
 
-        wk_codes, wk_scales = mx_tiles(const, "wk")
-        ks_codes, ks_scales = mx_tiles(const, "ks")
-        wq_codes, wq_scales = mx_tiles(const, "wq")
-        k_codes, k_scales = mx_tiles(const, "k")
-        quantise_rows(wk_raw, wk_codes, wk_scales)
-        quantise_rows(ks_raw, ks_codes, ks_scales)
-        quantise_rows(wq_raw, wq_codes, wq_scales)
-        project(wk_codes, wk_scales, ks_codes, ks_scales, bk_f, k_codes, k_scales, "r", 4)
+        def vector_add_bias(dst, acc, bias):
+            nc.vector.tensor_scalar(out=dst, in0=acc, scalar1=bias, scalar2=None, op0=ALU.add)
+
+        def new_planar():
+            return stage.tile([P, PACK, ROWS], BF16, name="planar", tag="planar")
+
+        def new_grouped_out():
+            return stage.tile([P, ROWS * PACK], BF16, name="grouped_out", tag="grouped_out", align_bytes=64)
+
+        def regroup_views(planar, grouped, first, count):
+            dst = grouped[:, first * L * PACK : (first + count) * L * PACK].rearrange("p (c i t) -> p c t i", i=4, t=PACK)
+            src = planar[:, :, first * L : (first + count) * L].rearrange("p t (c i) -> p c t i", i=4)
+            return dst, src
+
+        def regroup_on_vector(planar, grouped):
+            dst, src = regroup_views(planar, grouped, 0, GROUP)
+            nc.vector.tensor_copy(out=dst, in_=src)
+
+        def regroup_shared(planar, grouped):
+            for s in range(GPSIMD_SAMPLES):
+                nc.gpsimd.tensor_scalar(
+                    out=grouped[:, s * L * PACK : (s + 1) * L * PACK].rearrange("p (r t) -> p r t", t=PACK),
+                    in0=planar[:, :, s * L : (s + 1) * L].rearrange("p t r -> p r t"),
+                    scalar1=1.0,
+                    scalar2=0.0,
+                    op0=ALU.mult,
+                    op1=ALU.add,
+                )
+            dst, src = regroup_views(planar, grouped, GPSIMD_SAMPLES, GROUP - GPSIMD_SAMPLES)
+            nc.scalar.copy(out=dst, in_=src)
+
+        shared = (nc.vector.tensor_copy, nc.scalar.copy)
+        scalar_only = (nc.scalar.copy, nc.scalar.copy)
+
+        wk_mx = mx_tiles(const, "wk")
+        ks_mx = mx_tiles(const, "ks")
+        wq_mx = mx_tiles(const, "wq")
+        k_mx = mx_tiles(const, "k")
+        x_mx = {}
+        x_grouped = {}
+        q_mx = {}
+        q_grouped = {}
+
+        quantise(features_to_partitions(wk_raw, shared), wk_mx)
+        quantise(features_to_partitions(ks_raw, shared), ks_mx)
+        quantise(features_to_partitions(wq_raw, shared), wq_mx)
+        x_mx[0] = mx_tiles(stage, "x")
+        quantise(features_to_partitions(x_raw[0], shared), x_mx[0])
+
+        k_planar = new_planar()
+        for t in range(PACK):
+            acc = project_pass(wk_mx, ks_mx, t, "r", 4)
+            if t % 2 == 0:
+                vector_add_bias(k_planar[:, t, :], acc, bk_f[:, t : t + 1])
+            else:
+                scalar_add_bias(k_planar[:, t, :], acc, bk_f[:, t : t + 1])
+        x_grouped[1] = features_to_partitions(x_raw[1], scalar_only)
+        k_grouped = new_grouped_out()
+        regroup_on_vector(k_planar, k_grouped)
+        quantise(k_grouped, k_mx)
+
+        def project_queries_pass(g, planar, t):
+            acc = project_pass(wq_mx, x_mx[g], t, "proj", 2)
+            scalar_add_bias(planar[:, t, :], acc, bq_f[:, t : t + 1])
+
+        planar = new_planar()
+        for t in range(PACK):
+            project_queries_pass(0, planar, t)
+        x_mx[1] = mx_tiles(stage, "x")
+        quantise(x_grouped[1], x_mx[1])
+        q_grouped[0] = new_grouped_out()
+        regroup_on_vector(planar, q_grouped[0])
+        q_mx[0] = mx_tiles(stage, "q")
+        quantise(q_grouped[0], q_mx[0])
+        x_grouped[2] = features_to_partitions(x_raw[2], scalar_only)
+        planar = new_planar()
+        for t in range(PACK):
+            project_queries_pass(1, planar, t)
+        q_grouped[1] = new_grouped_out()
+        regroup_shared(planar, q_grouped[1])
+        x_mx[2] = mx_tiles(stage, "x")
+        quantise(x_grouped[2], x_mx[2])
 
         row_max = const.tile([P, BQ, BK], F32, name="row_max")
-        col_max = const.tile([P, BK, BQ], F32, name="col_max")
+        col_max = const.tile([P, BQ, BK], F32, name="col_max")
+        scores = {}
 
-        x_mx = {}
-        q_mx = {}
-
-        def stage_a(g):
-            x_mx[g] = mx_tiles(stage, "x")
-            quantise_rows(x_raw[g], x_mx[g][0], x_mx[g][1])
-
-        def stage_b(g):
-            q_mx[g] = mx_tiles(stage, "q")
-            project(wq_codes, wq_scales, x_mx[g][0], x_mx[g][1], bq_f, q_mx[g][0], q_mx[g][1], "proj", 2)
-
-        def stage_c(g):
-            q_codes, q_scales = q_mx[g]
-            for s in range(GROUP):
-                r = psum.tile([P, BK * L], F32, name="r", tag="r", bufs=4)
+        def fill_bank(g, j):
+            s = j // 2
+            q_codes = q_mx[g][0][:, s * L : (s + 1) * L]
+            q_scales = q_mx[g][1][:, s * L : (s + 1) * L]
+            bank = psum.tile([P, BK, L], F32, name="scores", tag="r", bufs=4)
+            if j % 2 == 0:
                 nc.tensor.matmul_mx(
-                    out=r,
-                    lhsT=q_codes[:, s * L : (s + 1) * L].bitcast(FP8X4),
-                    lhsT_scale=q_scales[:, s * L : (s + 1) * L],
-                    rhs=k_codes.bitcast(FP8X4),
-                    rhs_scale=k_scales,
+                    out=bank.rearrange("p b m -> p (b m)"),
+                    lhsT=q_codes.bitcast(FP8X4),
+                    lhsT_scale=q_scales,
+                    rhs=k_mx[0].bitcast(FP8X4),
+                    rhs_scale=k_mx[1],
                     start=True,
                     stop=True,
                 )
-                nc.vector.tensor_reduce(
-                    out=row_max[:, g * GROUP + s, :], in_=r.rearrange("p (b m) -> p b m", b=BK), axis=AXIS_X, op=ALU.max
-                )
-            for b in range(BK):
-                rt = psum.tile([P, ROWS], F32, name="rt", tag="r", bufs=4)
-                nc.tensor.matmul_mx(
-                    out=rt,
-                    lhsT=k_codes[:, b * L : (b + 1) * L].bitcast(FP8X4),
-                    lhsT_scale=k_scales[:, b * L : (b + 1) * L],
-                    rhs=q_codes.bitcast(FP8X4),
-                    rhs_scale=q_scales,
-                    start=True,
-                    stop=True,
-                )
-                nc.vector.tensor_reduce(
-                    out=col_max[:, b, g * GROUP : (g + 1) * GROUP],
-                    in_=rt.rearrange("p (a l) -> p a l", a=GROUP),
-                    axis=AXIS_X,
-                    op=ALU.max,
-                )
+            else:
+                for b in range(BK):
+                    nc.tensor.matmul_mx(
+                        out=bank[:, b, :],
+                        lhsT=k_mx[0][:, b * L : (b + 1) * L].bitcast(FP8X4),
+                        lhsT_scale=k_mx[1][:, b * L : (b + 1) * L],
+                        rhs=q_codes.bitcast(FP8X4),
+                        rhs_scale=q_scales,
+                        start=True,
+                        stop=True,
+                    )
+            scores[j] = bank
 
-        for step in range(N_GROUPS + 2):
-            if step < N_GROUPS:
-                stage_a(step)
-            if 1 <= step <= N_GROUPS:
-                stage_b(step - 1)
-            if step >= 2:
-                stage_c(step - 2)
+        def take_max(g, j):
+            maxima = row_max if j % 2 == 0 else col_max
+            nc.vector.tensor_reduce(out=maxima[:, g * GROUP + j // 2, :], in_=scores[j], axis=AXIS_X, op=ALU.max)
 
-        both = const.tile([P, BQ, BK], F32, name="both")
-        nc.vector.tensor_tensor(out=both, in0=row_max, in1=col_max.rearrange("p b a -> p a b"), op=ALU.add)
+        for g in range(N_GROUPS):
+            for j in range(BANKS // 2):
+                fill_bank(g, j)
+            if g + 3 < N_GROUPS:
+                x_grouped[g + 3] = features_to_partitions(x_raw[g + 3], scalar_only)
+            if g + 2 < N_GROUPS:
+                planar = new_planar()
+            for j in range(BANKS // 2):
+                take_max(g, j)
+                fill_bank(g, j + BANKS // 2)
+                if g + 2 < N_GROUPS:
+                    project_queries_pass(g + 2, planar, j)
+            if g + 2 < N_GROUPS:
+                q_grouped[g + 2] = new_grouped_out()
+                regroup_shared(planar, q_grouped[g + 2])
+            if g + 1 < N_GROUPS:
+                q_mx[g + 1] = mx_tiles(stage, "q")
+                quantise(q_grouped[g + 1], q_mx[g + 1])
+            if g + 3 < N_GROUPS:
+                x_mx[g + 3] = mx_tiles(stage, "x")
+                quantise(x_grouped[g + 3], x_mx[g + 3])
+            for j in range(BANKS // 2, BANKS):
+                take_max(g, j)
+
+        both = const.tile([P, BQ * BK], F32, name="both")
+        nc.vector.tensor_tensor(
+            out=both, in0=row_max.rearrange("p a b -> p (a b)"), in1=col_max.rearrange("p a b -> p (a b)"), op=ALU.add
+        )
         sums = psum.tile([P, BQ * BK], F32, name="sums", tag="r", bufs=4)
-        nc.tensor.matmul(out=sums, lhsT=ones, rhs=both.rearrange("p a b -> p (a b)"), start=True, stop=True)
+        nc.tensor.matmul(out=sums, lhsT=ones, rhs=both, start=True, stop=True)
         result = const.tile([P, BQ * BK], F32, name="result")
         nc.vector.tensor_scalar(
             out=result, in0=sums, scalar1=gain[:, 0:1], scalar2=1.0 / (2 * L), op0=ALU.mult, op1=ALU.mult

@@ -15,12 +15,16 @@ AXIS_X = mybir.AxisListType.X
 P = 128
 PACK = 4
 BQ, BK, L, D = 64, 4, 128, 512
-GROUP = 4
-ROWS = GROUP * L
-N_GROUPS = BQ // GROUP
 WORDS = D // 2
-BANKS = 2 * GROUP
-GPSIMD_SAMPLES = 2
+UNIT = 2
+ROWS = UNIT * L
+N_UNITS = BQ // UNIT
+HALVES = D // ROWS
+
+LEAD_TRANSPOSE = 4
+LEAD_QUANTISE_X = 3
+LEAD_PROJECT = 2
+LEAD_QUANTISE_Q = 1
 
 FLOPS = 2 * D * D * (BQ + BK) * L + 2 * (BQ * L) * (BK * L) * D
 
@@ -29,27 +33,24 @@ def tile_attention_pa_t_kernel(tc, query_states, key_states, Wq, bq, Wk, bk, log
     nc = tc.nc
     with ExitStack() as stack:
         const = stack.enter_context(tc.tile_pool(name="const", bufs=1))
-        xpool = stack.enter_context(tc.tile_pool(name="xpool", bufs=N_GROUPS))
-        stage = stack.enter_context(tc.tile_pool(name="stage", bufs=3))
+        xpool = stack.enter_context(tc.tile_pool(name="xpool", bufs=N_UNITS))
+        stage = stack.enter_context(tc.tile_pool(name="stage", bufs=4))
         psum = stack.enter_context(tc.psum_pool(name="psum", bufs=2))
         stack.enter_context(tc.manual_schedule())
 
-        wk_raw = const.tile([P, GROUP * D], BF16, name="wk_raw")
-        ks_raw = const.tile([P, GROUP * D], BF16, name="ks_raw")
-        wq_raw = const.tile([P, GROUP * D], BF16, name="wq_raw")
-        nc.sync.dma_start(out=wk_raw, in_=Wk.rearrange("(m t) d -> m (t d)", t=PACK))
-        nc.sync.dma_start(
-            out=ks_raw.rearrange("p (s d) -> p s d", s=GROUP), in_=key_states.rearrange("s l d -> l s d")
-        )
-        nc.sync.dma_start(out=wq_raw, in_=Wq.rearrange("(m t) d -> m (t d)", t=PACK))
-        x_raw = []
-        for g in range(N_GROUPS):
-            xg = xpool.tile([P, GROUP * D], BF16, name="x_raw", tag="x_raw")
-            nc.sync.dma_start(
-                out=xg.rearrange("p (s d) -> p s d", s=GROUP),
-                in_=query_states[g * GROUP : (g + 1) * GROUP].rearrange("s l d -> l s d"),
-            )
-            x_raw.append(xg)
+        def load(pool, name, rows):
+            raw = pool.tile([P, UNIT * D], BF16, name=name, tag=name)
+            nc.sync.dma_start(out=raw.rearrange("p (s d) -> p s d", s=UNIT), in_=rows)
+            return raw
+
+        wk_rows = Wk.rearrange("(m t) d -> m t d", t=PACK)
+        wq_rows = Wq.rearrange("(m t) d -> m t d", t=PACK)
+        ks_rows = key_states.rearrange("s l d -> l s d")
+        xs_rows = query_states.rearrange("s l d -> l s d")
+        wk_raw = [load(const, "wk_raw%d" % h, wk_rows[:, h * UNIT : (h + 1) * UNIT, :]) for h in range(HALVES)]
+        ks_raw = [load(const, "ks_raw%d" % h, ks_rows[:, h * UNIT : (h + 1) * UNIT, :]) for h in range(HALVES)]
+        wq_raw = [load(const, "wq_raw%d" % h, wq_rows[:, h * UNIT : (h + 1) * UNIT, :]) for h in range(HALVES)]
+        x_raw = [load(xpool, "x_raw", xs_rows[:, u * UNIT : (u + 1) * UNIT, :]) for u in range(N_UNITS)]
 
         bk_bf = const.tile([P, PACK], BF16, name="bk_bf")
         bq_bf = const.tile([P, PACK], BF16, name="bq_bf")
@@ -69,45 +70,55 @@ def tile_attention_pa_t_kernel(tc, query_states, key_states, Wq, bq, Wk, bk, log
         nc.vector.tensor_copy(out=bk_f, in_=bk_bf)
         nc.vector.tensor_copy(out=bq_f, in_=bq_bf)
 
-        def mx_tiles(pool, name):
-            codes = pool.tile([P, ROWS], U32, name=name + "_codes", tag=name + "_codes", align_bytes=64)
-            scales = pool.tile([P, ROWS], U8, name=name + "_scales", tag=name + "_scales", align_bytes=64)
+        def mx_tiles(pool, name, columns):
+            codes = pool.tile([P, columns], U32, name=name + "_codes", tag=name + "_codes", align_bytes=64)
+            scales = pool.tile([P, columns], U8, name=name + "_scales", tag=name + "_scales", align_bytes=64)
             return codes, scales
+
+        def columns_of(operand, first, count):
+            return operand[0][:, first : first + count], operand[1][:, first : first + count]
 
         def quantise(grouped, operand):
             nc.vector.quantize_mx(out=operand[0].bitcast(FP8X4), scales=operand[1], in_=grouped)
 
-        def features_to_partitions(raw, copies):
-            raw_words = raw.bitcast(F32)
-            grouped = stage.tile([P, ROWS * PACK], BF16, name="grouped_in", tag="grouped_in", align_bytes=64)
-            grouped_words = grouped.bitcast(F32).rearrange("p (s r u) -> p s r u", s=GROUP, u=2)
-            for half in range(2):
-                bank = psum.tile([P, 2, 2, P], F32, name="xt", tag="xt")
-                for s in range(2):
-                    for u in range(2):
-                        first = (2 * half + s) * WORDS + u * P
-                        nc.tensor.transpose(bank[:, s, u, :], raw_words[:, first : first + P], ident)
-                copies[half](out=grouped_words[:, 2 * half : 2 * half + 2], in_=bank.rearrange("p s u r -> p s r u"))
-            return grouped
-
-        def project_pass(weights, rows, t, tag, bufs):
-            acc = psum.tile([P, ROWS], F32, name="acc", tag=tag, bufs=bufs)
+        def multiply(acc, stationary, moving):
             nc.tensor.matmul_mx(
                 out=acc,
-                lhsT=weights[0][:, t * P : (t + 1) * P].bitcast(FP8X4),
-                lhsT_scale=weights[1][:, t * P : (t + 1) * P],
-                rhs=rows[0].bitcast(FP8X4),
-                rhs_scale=rows[1],
+                lhsT=stationary[0].bitcast(FP8X4),
+                lhsT_scale=stationary[1],
+                rhs=moving[0].bitcast(FP8X4),
+                rhs_scale=moving[1],
                 start=True,
                 stop=True,
             )
-            return acc
+
+        def features_to_partitions(raw, copy, tag, bufs):
+            raw_words = raw.bitcast(F32)
+            bank = psum.tile([P, UNIT, 2, P], F32, name="xt", tag=tag, bufs=bufs)
+            for s in range(UNIT):
+                for u in range(2):
+                    first = s * WORDS + u * P
+                    nc.tensor.transpose(bank[:, s, u, :], raw_words[:, first : first + P], ident)
+            grouped = stage.tile([P, ROWS * PACK], BF16, name="grouped_in", tag="grouped_in", align_bytes=64)
+            copy(
+                out=grouped.bitcast(F32).rearrange("p (s r u) -> p s r u", s=UNIT, u=2),
+                in_=bank.rearrange("p s u r -> p s r u"),
+            )
+            return grouped
 
         def scalar_add_bias(dst, acc, bias):
             nc.scalar.activation(out=dst, in_=acc, func=ACT.Identity, bias=bias, scale=1.0)
 
         def vector_add_bias(dst, acc, bias):
             nc.vector.tensor_scalar(out=dst, in0=acc, scalar1=bias, scalar2=None, op0=ALU.add)
+
+        def project_pair(weights, rows, bias, planar, pair, add_bias, tag, bufs):
+            bank = psum.tile([P, 2, ROWS], F32, name="proj", tag=tag, bufs=bufs)
+            for i in range(2):
+                multiply(bank[:, i, :], columns_of(weights, (2 * pair + i) * P, P), rows)
+            for i in range(2):
+                t = 2 * pair + i
+                add_bias[i](planar[:, t, :], bank[:, i, :], bias[:, t : t + 1])
 
         def new_planar():
             return stage.tile([P, PACK, ROWS], BF16, name="planar", tag="planar")
@@ -120,141 +131,101 @@ def tile_attention_pa_t_kernel(tc, query_states, key_states, Wq, bq, Wk, bk, log
             src = planar[:, :, first * L : (first + count) * L].rearrange("p t (c i) -> p c t i", i=4)
             return dst, src
 
-        def regroup_on_vector(planar, grouped):
-            dst, src = regroup_views(planar, grouped, 0, GROUP)
-            nc.vector.tensor_copy(out=dst, in_=src)
+        wk_mx = mx_tiles(const, "wk", D)
+        ks_mx = mx_tiles(const, "ks", D)
+        wq_mx = mx_tiles(const, "wq", D)
+        k_mx = mx_tiles(const, "k", D)
+        half_copy = (nc.vector.tensor_copy, nc.scalar.copy)
+        for raws, operand in ((wk_raw, wk_mx), (ks_raw, ks_mx), (wq_raw, wq_mx)):
+            grouped_halves = [features_to_partitions(raws[h], half_copy[h], "r", 4) for h in range(HALVES)]
+            for h in range(HALVES):
+                quantise(grouped_halves[h], columns_of(operand, h * ROWS, ROWS))
 
-        def regroup_shared(planar, grouped):
-            for s in range(GPSIMD_SAMPLES):
-                nc.gpsimd.tensor_scalar(
-                    out=grouped[:, s * L * PACK : (s + 1) * L * PACK].rearrange("p (r t) -> p r t", t=PACK),
-                    in0=planar[:, :, s * L : (s + 1) * L].rearrange("p t r -> p r t"),
-                    scalar1=1.0,
-                    scalar2=0.0,
-                    op0=ALU.mult,
-                    op1=ALU.add,
+        def project_keys(h):
+            planar = new_planar()
+            for pair in range(2):
+                project_pair(
+                    wk_mx, columns_of(ks_mx, h * ROWS, ROWS), bk_f, planar, pair, (vector_add_bias, scalar_add_bias), "r", 4
                 )
-            dst, src = regroup_views(planar, grouped, GPSIMD_SAMPLES, GROUP - GPSIMD_SAMPLES)
-            nc.scalar.copy(out=dst, in_=src)
-
-        shared = (nc.vector.tensor_copy, nc.scalar.copy)
-        scalar_only = (nc.scalar.copy, nc.scalar.copy)
-
-        wk_mx = mx_tiles(const, "wk")
-        ks_mx = mx_tiles(const, "ks")
-        wq_mx = mx_tiles(const, "wq")
-        k_mx = mx_tiles(const, "k")
-        x_mx = {}
-        x_grouped = {}
-        q_mx = {}
-        q_grouped = {}
-
-        quantise(features_to_partitions(wk_raw, shared), wk_mx)
-        quantise(features_to_partitions(ks_raw, shared), ks_mx)
-        quantise(features_to_partitions(wq_raw, shared), wq_mx)
-        x_mx[0] = mx_tiles(stage, "x")
-        quantise(features_to_partitions(x_raw[0], shared), x_mx[0])
-
-        k_planar = new_planar()
-        for t in range(PACK):
-            acc = project_pass(wk_mx, ks_mx, t, "r", 4)
-            if t % 2 == 0:
-                vector_add_bias(k_planar[:, t, :], acc, bk_f[:, t : t + 1])
-            else:
-                scalar_add_bias(k_planar[:, t, :], acc, bk_f[:, t : t + 1])
-        x_grouped[1] = features_to_partitions(x_raw[1], scalar_only)
-        k_grouped = new_grouped_out()
-        regroup_on_vector(k_planar, k_grouped)
-        quantise(k_grouped, k_mx)
-
-        def project_queries_pass(g, planar, t):
-            acc = project_pass(wq_mx, x_mx[g], t, "proj", 2)
-            scalar_add_bias(planar[:, t, :], acc, bq_f[:, t : t + 1])
-
-        planar = new_planar()
-        for t in range(PACK):
-            project_queries_pass(0, planar, t)
-        x_mx[1] = mx_tiles(stage, "x")
-        quantise(x_grouped[1], x_mx[1])
-        q_grouped[0] = new_grouped_out()
-        regroup_on_vector(planar, q_grouped[0])
-        q_mx[0] = mx_tiles(stage, "q")
-        quantise(q_grouped[0], q_mx[0])
-        x_grouped[2] = features_to_partitions(x_raw[2], scalar_only)
-        planar = new_planar()
-        for t in range(PACK):
-            project_queries_pass(1, planar, t)
-        q_grouped[1] = new_grouped_out()
-        regroup_shared(planar, q_grouped[1])
-        x_mx[2] = mx_tiles(stage, "x")
-        quantise(x_grouped[2], x_mx[2])
+            grouped = new_grouped_out()
+            dst, src = regroup_views(planar, grouped, 0, UNIT)
+            nc.vector.tensor_copy(out=dst, in_=src)
+            quantise(grouped, columns_of(k_mx, h * ROWS, ROWS))
 
         row_max = const.tile([P, BQ, BK], F32, name="row_max")
         col_max = const.tile([P, BQ, BK], F32, name="col_max")
+        x_grouped = {}
+        x_mx = {}
+        q_planar = {}
+        q_grouped = {}
+        q_mx = {}
         scores = {}
+        BANKS = 2 * UNIT
 
-        def fill_bank(g, j):
-            s = j // 2
-            q_codes = q_mx[g][0][:, s * L : (s + 1) * L]
-            q_scales = q_mx[g][1][:, s * L : (s + 1) * L]
+        def fill_bank(u, j):
+            q_sample = columns_of(q_mx[u], (j // 2) * L, L)
             bank = psum.tile([P, BK, L], F32, name="scores", tag="r", bufs=4)
             if j % 2 == 0:
-                nc.tensor.matmul_mx(
-                    out=bank.rearrange("p b m -> p (b m)"),
-                    lhsT=q_codes.bitcast(FP8X4),
-                    lhsT_scale=q_scales,
-                    rhs=k_mx[0].bitcast(FP8X4),
-                    rhs_scale=k_mx[1],
-                    start=True,
-                    stop=True,
-                )
+                multiply(bank.rearrange("p b m -> p (b m)"), q_sample, k_mx)
             else:
                 for b in range(BK):
-                    nc.tensor.matmul_mx(
-                        out=bank[:, b, :],
-                        lhsT=k_mx[0][:, b * L : (b + 1) * L].bitcast(FP8X4),
-                        lhsT_scale=k_mx[1][:, b * L : (b + 1) * L],
-                        rhs=q_codes.bitcast(FP8X4),
-                        rhs_scale=q_scales,
-                        start=True,
-                        stop=True,
-                    )
+                    multiply(bank[:, b, :], columns_of(k_mx, b * L, L), q_sample)
             scores[j] = bank
 
-        def take_max(g, j):
+        def take_max(u, j):
             maxima = row_max if j % 2 == 0 else col_max
-            nc.vector.tensor_reduce(out=maxima[:, g * GROUP + j // 2, :], in_=scores[j], axis=AXIS_X, op=ALU.max)
+            nc.vector.tensor_reduce(out=maxima[:, u * UNIT + j // 2, :], in_=scores[j], axis=AXIS_X, op=ALU.max)
 
-        for g in range(N_GROUPS):
-            for j in range(BANKS // 2):
-                fill_bank(g, j)
-            if g + 3 < N_GROUPS:
-                x_grouped[g + 3] = features_to_partitions(x_raw[g + 3], scalar_only)
-            if g + 2 < N_GROUPS:
-                planar = new_planar()
-            for j in range(BANKS // 2):
-                take_max(g, j)
-                fill_bank(g, j + BANKS // 2)
-                if g + 2 < N_GROUPS:
-                    project_queries_pass(g + 2, planar, j)
-            if g + 2 < N_GROUPS:
-                q_grouped[g + 2] = new_grouped_out()
-                regroup_shared(planar, q_grouped[g + 2])
-            if g + 1 < N_GROUPS:
-                q_mx[g + 1] = mx_tiles(stage, "q")
-                quantise(q_grouped[g + 1], q_mx[g + 1])
-            if g + 3 < N_GROUPS:
-                x_mx[g + 3] = mx_tiles(stage, "x")
-                quantise(x_grouped[g + 3], x_mx[g + 3])
-            for j in range(BANKS // 2, BANKS):
-                take_max(g, j)
+        def regroup_queries(planar, grouped):
+            nc.gpsimd.tensor_scalar(
+                out=grouped[:, : L * PACK].rearrange("p (r t) -> p r t", t=PACK),
+                in0=planar[:, :, :L].rearrange("p t r -> p r t"),
+                scalar1=1.0,
+                scalar2=0.0,
+                op0=ALU.mult,
+                op1=ALU.add,
+            )
+            dst, src = regroup_views(planar, grouped, 1, UNIT - 1)
+            nc.scalar.copy(out=dst, in_=src)
 
-        both = const.tile([P, BQ * BK], F32, name="both")
-        nc.vector.tensor_tensor(
-            out=both, in0=row_max.rearrange("p a b -> p (a b)"), in1=col_max.rearrange("p a b -> p (a b)"), op=ALU.add
-        )
+        def exists(u):
+            return 0 <= u < N_UNITS
+
+        for u in range(-LEAD_TRANSPOSE, N_UNITS):
+            if u == -LEAD_TRANSPOSE + 1:
+                project_keys(0)
+            if u == -LEAD_TRANSPOSE + 2:
+                project_keys(1)
+            ut, ux, up, uq = u + LEAD_TRANSPOSE, u + LEAD_QUANTISE_X, u + LEAD_PROJECT, u + LEAD_QUANTISE_Q
+            if exists(u):
+                for j in range(BANKS // 2):
+                    fill_bank(u, j)
+            if exists(ut):
+                x_grouped[ut] = features_to_partitions(x_raw[ut], nc.scalar.copy, "xt", 2)
+            if exists(up):
+                q_planar[up] = new_planar()
+            for j in range(BANKS // 2):
+                if exists(u):
+                    take_max(u, j)
+                    fill_bank(u, j + BANKS // 2)
+                if exists(up):
+                    project_pair(wq_mx, x_mx[up], bq_f, q_planar[up], j, (scalar_add_bias, scalar_add_bias), "proj", 2)
+            if exists(up):
+                q_grouped[up] = new_grouped_out()
+                regroup_queries(q_planar[up], q_grouped[up])
+            if exists(uq):
+                q_mx[uq] = mx_tiles(stage, "q", ROWS)
+                quantise(q_grouped[uq], q_mx[uq])
+            if exists(ux):
+                x_mx[ux] = mx_tiles(stage, "x", ROWS)
+                quantise(x_grouped[ux], x_mx[ux])
+            if exists(u):
+                for j in range(BANKS // 2, BANKS):
+                    take_max(u, j)
+
         sums = psum.tile([P, BQ * BK], F32, name="sums", tag="r", bufs=4)
-        nc.tensor.matmul(out=sums, lhsT=ones, rhs=both, start=True, stop=True)
+        nc.tensor.matmul(out=sums, lhsT=ones, rhs=row_max.rearrange("p a b -> p (a b)"), start=True, stop=False)
+        nc.tensor.matmul(out=sums, lhsT=ones, rhs=col_max.rearrange("p a b -> p (a b)"), start=False, stop=True)
         result = const.tile([P, BQ * BK], F32, name="result")
         nc.vector.tensor_scalar(
             out=result, in0=sums, scalar1=gain[:, 0:1], scalar2=1.0 / (2 * L), op0=ALU.mult, op1=ALU.mult

@@ -36,7 +36,6 @@ def tile_attention_pa_t_kernel(tc, query_states, key_states, Wq, bq, Wk, bk, log
         xpool = stack.enter_context(tc.tile_pool(name="xpool", bufs=N_UNITS))
         stage = stack.enter_context(tc.tile_pool(name="stage", bufs=4))
         psum = stack.enter_context(tc.psum_pool(name="psum", bufs=2))
-        stack.enter_context(tc.manual_schedule())
 
         def load(pool, name, rows):
             raw = pool.tile([P, UNIT * D], BF16, name=name, tag=name)

@@ -123,7 +123,7 @@ def tile_attention_pa_t_kernel(tc, query_states, key_states, Wq, bq, Wk, bk, log
             return stage.tile([P, PACK, ROWS], BF16, name="planar", tag="planar")
 
         def new_grouped_out():
-            return stage.tile([P, ROWS * PACK], BF16, name="grouped_out", tag="grouped_out", align_bytes=64)
+            return stage.tile([P, ROWS * PACK], BF16, name="grouped_out", tag="grouped_out", bufs=1, align_bytes=64)
 
         def regroup_views(planar, grouped, first, count):
             dst = grouped[:, first * L * PACK : (first + count) * L * PACK].rearrange("p (c i t) -> p c t i", i=4, t=PACK)
@@ -209,15 +209,15 @@ def tile_attention_pa_t_kernel(tc, query_states, key_states, Wq, bq, Wk, bk, log
                     fill_bank(u, j + BANKS // 2)
                 if exists(up):
                     project_pair(wq_mx, x_mx[up], bq_f, q_planar[up], j, (scalar_add_bias, scalar_add_bias), "proj", 2)
-            if exists(up):
-                q_grouped[up] = new_grouped_out()
-                regroup_queries(q_planar[up], q_grouped[up])
-            if exists(uq):
-                q_mx[uq] = mx_tiles(stage, "q", ROWS)
-                quantise(q_grouped[uq], q_mx[uq])
             if exists(ux):
                 x_mx[ux] = mx_tiles(stage, "x", ROWS)
                 quantise(x_grouped[ux], x_mx[ux])
+            if exists(uq):
+                q_mx[uq] = mx_tiles(stage, "q", ROWS)
+                quantise(q_grouped[uq], q_mx[uq])
+            if exists(up):
+                q_grouped[up] = new_grouped_out()
+                regroup_queries(q_planar[up], q_grouped[up])
             if exists(u):
                 for j in range(BANKS // 2, BANKS):
                     take_max(u, j)

@@ -162,18 +162,20 @@ def tile_attention_pa_t_kernel(tc, query_states, key_states, Wq, bq, Wk, bk, log
         BANKS = 2 * UNIT
 
         def fill_bank(u, j):
-            q_sample = columns_of(q_mx[u], (j // 2) * L, L)
-            bank = psum.tile([P, BK, L], F32, name="scores", tag="r", bufs=4)
+            bank = psum.tile([P, 2, 2, L], F32, name="scores", tag="r", bufs=4)
             if j % 2 == 0:
-                multiply(bank.rearrange("p b m -> p (b m)"), q_sample, k_mx)
+                multiply(bank.rearrange("p c d m -> p (c d m)"), columns_of(q_mx[u], (j // 2) * L, L), k_mx)
             else:
-                for b in range(BK):
-                    multiply(bank[:, b, :], columns_of(k_mx, b * L, L), q_sample)
+                for i in range(2):
+                    multiply(bank[:, i, :, :].rearrange("p a l -> p (a l)"), columns_of(k_mx, (j - 1 + i) * L, L), q_mx[u])
             scores[j] = bank
 
         def take_max(u, j):
-            maxima = row_max if j % 2 == 0 else col_max
-            nc.vector.tensor_reduce(out=maxima[:, u * UNIT + j // 2, :], in_=scores[j], axis=AXIS_X, op=ALU.max)
+            if j % 2 == 0:
+                maxima = row_max[:, u * UNIT + j // 2, :].rearrange("p (c d) -> p c d", c=2)
+            else:
+                maxima = col_max[:, u * UNIT : (u + 1) * UNIT, j - 1 : j + 1].rearrange("p a b -> p b a")
+            nc.vector.tensor_reduce(out=maxima, in_=scores[j], axis=AXIS_X, op=ALU.max)
 
         def regroup_queries(planar, grouped):
             nc.gpsimd.tensor_scalar(

@@ -21,6 +21,11 @@ ROWS = UNIT * L
 N_UNITS = BQ // UNIT
 HALVES = D // ROWS
 
+POOL_ROWS = 192
+SPLIT = BK * L // 2
+
+FIRST_PAIRED = 2
+
 LEAD_TRANSPOSE = 4
 LEAD_QUANTISE_X = 3
 LEAD_PROJECT = 2
@@ -46,10 +51,18 @@ def tile_attention_pa_t_kernel(tc, query_states, key_states, Wq, bq, Wk, bk, log
         wq_rows = Wq.rearrange("(m t) d -> m t d", t=PACK)
         ks_rows = key_states.rearrange("s l d -> l s d")
         xs_rows = query_states.rearrange("s l d -> l s d")
-        wk_raw = [load(const, "wk_raw%d" % h, wk_rows[:, h * UNIT : (h + 1) * UNIT, :]) for h in range(HALVES)]
-        ks_raw = [load(const, "ks_raw%d" % h, ks_rows[:, h * UNIT : (h + 1) * UNIT, :]) for h in range(HALVES)]
-        wq_raw = [load(const, "wq_raw%d" % h, wq_rows[:, h * UNIT : (h + 1) * UNIT, :]) for h in range(HALVES)]
-        x_raw = [load(xpool, "x_raw", xs_rows[:, u * UNIT : (u + 1) * UNIT, :]) for u in range(N_UNITS)]
+        def load_half(name, rows, h):
+            return load(const, "%s_raw%d" % (name, h), rows[:, h * UNIT : (h + 1) * UNIT, :])
+
+        def load_x(u):
+            return load(xpool, "x_raw", xs_rows[:, u * UNIT : (u + 1) * UNIT, :])
+
+        wk_raw = [load_half("wk", wk_rows, h) for h in range(HALVES)]
+        ks_raw = [load_half("ks", ks_rows, 0)]
+        wq_raw = [load_half("wq", wq_rows, h) for h in range(HALVES)]
+        x_raw = [load_x(0)]
+        ks_raw.append(load_half("ks", ks_rows, 1))
+        x_raw.extend([load_x(u) for u in range(1, N_UNITS)])
 
         bk_bf = const.tile([P, PACK], BF16, name="bk_bf")
         bq_bf = const.tile([P, PACK], BF16, name="bq_bf")
@@ -62,12 +75,6 @@ def tile_attention_pa_t_kernel(tc, query_states, key_states, Wq, bq, Wk, bk, log
         make_identity(nc, ident)
         ones = const.tile([P, P], F32, name="ones")
         nc.gpsimd.memset(ones, 1.0)
-        gain = const.tile([P, 1], F32, name="gain")
-        nc.scalar.activation(out=gain, in_=ls_bf, func=ACT.Exp)
-        bk_f = const.tile([P, PACK], F32, name="bk_f")
-        bq_f = const.tile([P, PACK], F32, name="bq_f")
-        nc.vector.tensor_copy(out=bk_f, in_=bk_bf)
-        nc.vector.tensor_copy(out=bq_f, in_=bq_bf)
 
         def mx_tiles(pool, name, columns):
             codes = pool.tile([P, columns], U32, name=name + "_codes", tag=name + "_codes", align_bytes=64)
@@ -80,15 +87,15 @@ def tile_attention_pa_t_kernel(tc, query_states, key_states, Wq, bq, Wk, bk, log
         def quantise(grouped, operand):
             nc.vector.quantize_mx(out=operand[0].bitcast(FP8X4), scales=operand[1], in_=grouped)
 
-        def multiply(acc, stationary, moving):
+        def multiply(acc, stationary, moving, start=True, stop=True):
             nc.tensor.matmul_mx(
                 out=acc,
                 lhsT=stationary[0].bitcast(FP8X4),
                 lhsT_scale=stationary[1],
                 rhs=moving[0].bitcast(FP8X4),
                 rhs_scale=moving[1],
-                start=True,
-                stop=True,
+                start=start,
+                stop=stop,
             )
 
         def features_to_partitions(raw, copy, tag, bufs):
@@ -98,7 +105,7 @@ def tile_attention_pa_t_kernel(tc, query_states, key_states, Wq, bq, Wk, bk, log
                 for u in range(2):
                     first = s * WORDS + u * P
                     nc.tensor.transpose(bank[:, s, u, :], raw_words[:, first : first + P], ident)
-            grouped = stage.tile([P, ROWS * PACK], BF16, name="grouped_in", tag="grouped_in", align_bytes=64)
+            grouped = stage.tile([P, ROWS * PACK], BF16, name="grouped_in", tag="grouped_in", bufs=6, align_bytes=64)
             copy(
                 out=grouped.bitcast(F32).rearrange("p (s r u) -> p s r u", s=UNIT, u=2),
                 in_=bank.rearrange("p s u r -> p s r u"),
@@ -107,9 +114,6 @@ def tile_attention_pa_t_kernel(tc, query_states, key_states, Wq, bq, Wk, bk, log
 
         def scalar_add_bias(dst, acc, bias):
             nc.scalar.activation(out=dst, in_=acc, func=ACT.Identity, bias=bias, scale=1.0)
-
-        def vector_add_bias(dst, acc, bias):
-            nc.vector.tensor_scalar(out=dst, in0=acc, scalar1=bias, scalar2=None, op0=ALU.add)
 
         def project_pair(weights, rows, bias, planar, pair, add_bias, tag, bufs):
             bank = psum.tile([P, 2, ROWS], F32, name="proj", tag=tag, bufs=bufs)
@@ -125,31 +129,54 @@ def tile_attention_pa_t_kernel(tc, query_states, key_states, Wq, bq, Wk, bk, log
         def new_grouped_out():
             return stage.tile([P, ROWS * PACK], BF16, name="grouped_out", tag="grouped_out", bufs=1, align_bytes=64)
 
-        def regroup_views(planar, grouped, first, count):
-            dst = grouped[:, first * L * PACK : (first + count) * L * PACK].rearrange("p (c i t) -> p c t i", i=4, t=PACK)
-            src = planar[:, :, first * L : (first + count) * L].rearrange("p t (c i) -> p c t i", i=4)
-            return dst, src
-
         wk_mx = mx_tiles(const, "wk", D)
         ks_mx = mx_tiles(const, "ks", D)
         wq_mx = mx_tiles(const, "wq", D)
         k_mx = mx_tiles(const, "k", D)
-        half_copy = (nc.vector.tensor_copy, nc.scalar.copy)
-        for raws, operand in ((wk_raw, wk_mx), (ks_raw, ks_mx), (wq_raw, wq_mx)):
-            grouped_halves = [features_to_partitions(raws[h], half_copy[h], "r", 4) for h in range(HALVES)]
-            for h in range(HALVES):
-                quantise(grouped_halves[h], columns_of(operand, h * ROWS, ROWS))
+        split_mx = [mx_tiles(const, "split%d" % i, SPLIT) for i in range(3)]
+        split_grouped = []
+        for i in range(3):
+            half = const.tile([P, SPLIT * PACK], BF16, name="split_grouped%d" % i, align_bytes=64)
+            split_grouped.append(half)
+        def spread(raw, copy):
+            return features_to_partitions(raw, copy, "r", 4)
+
+        def half_of(operand, h):
+            return columns_of(operand, h * ROWS, ROWS)
 
         def project_keys(h):
-            planar = new_planar()
-            for pair in range(2):
-                project_pair(
-                    wk_mx, columns_of(ks_mx, h * ROWS, ROWS), bk_f, planar, pair, (vector_add_bias, scalar_add_bias), "r", 4
+            grouped = stage.tile([P, ROWS * PACK], BF16, name="grouped_k", tag="grouped_k", bufs=2, align_bytes=64)
+            for s in range(UNIT):
+                bank = psum.tile([P, PACK, L], F32, name="keys", tag="r", bufs=4)
+                for t in range(PACK):
+                    multiply(bank[:, t, :], columns_of(wk_mx, t * P, P), columns_of(ks_mx, (h * UNIT + s) * L, L))
+                nc.vector.tensor_tensor(
+                    out=grouped[:, s * L * PACK : (s + 1) * L * PACK].rearrange("p (m t) -> p m t", t=PACK),
+                    in0=bank.rearrange("p t m -> p m t"),
+                    in1=bk_bf.unsqueeze(1).to_broadcast([P, L, PACK]),
+                    op=ALU.add,
                 )
-            grouped = new_grouped_out()
-            dst, src = regroup_views(planar, grouped, 0, UNIT)
-            nc.vector.tensor_copy(out=dst, in_=src)
-            quantise(grouped, columns_of(k_mx, h * ROWS, ROWS))
+            quantise(grouped, half_of(k_mx, h))
+            by_half = grouped.rearrange("p (b c v) -> p b c v", b=UNIT, c=2)
+            for i in range(3):
+                nc.gpsimd.tensor_scalar(
+                    out=split_grouped[i][:, h * ROWS * 2 : (h + 1) * ROWS * 2].rearrange("p (b v) -> p b v", b=UNIT),
+                    in0=by_half[:, :, min(i, 1), :],
+                    scalar1=-1.0 if i == 2 else 1.0,
+                    scalar2=0.0,
+                    op0=ALU.mult,
+                    op1=ALU.add,
+                )
+
+        wk_grouped = [spread(wk_raw[0], nc.vector.tensor_copy), spread(wk_raw[1], nc.scalar.copy)]
+        ks_grouped = [spread(ks_raw[0], nc.vector.tensor_copy)]
+        for h in range(HALVES):
+            quantise(wk_grouped[h], half_of(wk_mx, h))
+        quantise(ks_grouped[0], half_of(ks_mx, 0))
+        wq_grouped = [spread(wq_raw[0], nc.scalar.copy), spread(wq_raw[1], nc.scalar.copy)]
+        project_keys(0)
+        for h in range(HALVES):
+            quantise(wq_grouped[h], half_of(wq_mx, h))
 
         row_max = const.tile([P, BQ, BK], F32, name="row_max")
         col_max = const.tile([P, BQ, BK], F32, name="col_max")
@@ -179,38 +206,75 @@ def tile_attention_pa_t_kernel(tc, query_states, key_states, Wq, bq, Wk, bk, log
 
         def regroup_queries(planar, grouped):
             nc.gpsimd.tensor_scalar(
-                out=grouped[:, : L * PACK].rearrange("p (r t) -> p r t", t=PACK),
-                in0=planar[:, :, :L].rearrange("p t r -> p r t"),
+                out=grouped[:, : POOL_ROWS * PACK].rearrange("p (r t) -> p r t", t=PACK),
+                in0=planar[:, :, :POOL_ROWS].rearrange("p t r -> p r t"),
                 scalar1=1.0,
                 scalar2=0.0,
                 op0=ALU.mult,
                 op1=ALU.add,
             )
-            dst, src = regroup_views(planar, grouped, 1, UNIT - 1)
-            nc.scalar.copy(out=dst, in_=src)
+            nc.scalar.copy(
+                out=grouped[:, POOL_ROWS * PACK :].rearrange("p (c i t) -> p c t i", i=4, t=PACK),
+                in_=planar[:, :, POOL_ROWS:].rearrange("p t (c i) -> p c t i", i=4),
+            )
 
         def exists(u):
             return 0 <= u < N_UNITS
 
+        paired_sums = {}
+        parts_of = {}
+
+        def paired(u):
+            return FIRST_PAIRED <= u < N_UNITS - 2
+
+        def fill_paired(u):
+            q_sample = columns_of(q_mx[u], L, L)
+            bank = psum.tile([P, 2, SPLIT], F32, name="scores", tag="r", bufs=4)
+            multiply(bank[:, 0, :], q_sample, split_mx[0], stop=False)
+            multiply(bank[:, 0, :], q_sample, split_mx[2], start=False)
+            multiply(bank[:, 1, :], q_sample, split_mx[1])
+            scores[2] = bank
+
+        def part(u):
+            parts = stage.tile([P, 2, SPLIT], F32, name="parts", tag="parts")
+            nc.scalar.activation(out=parts[:, 0, :], in_=scores[2][:, 0, :], func=ACT.Relu)
+            nc.scalar.copy(out=parts[:, 1, :], in_=scores[2][:, 1, :])
+            parts_of[u] = parts
+
+        def add_parts(u):
+            parts = parts_of[u]
+            paired_sum = stage.tile([P, SPLIT], F32, name="paired_sum", tag="paired_sum")
+            nc.gpsimd.tensor_tensor(out=paired_sum, in0=parts[:, 0, :], in1=parts[:, 1, :], op=ALU.add)
+            paired_sums[u] = paired_sum
+
+        def take_paired_max(u):
+            nc.vector.tensor_reduce(
+                out=row_max[:, u * UNIT + 1, :],
+                in_=paired_sums[u].rearrange("p (b m) -> p b m", b=BK),
+                axis=AXIS_X,
+                op=ALU.max,
+            )
+
         for u in range(-LEAD_TRANSPOSE, N_UNITS):
-            if u == -LEAD_TRANSPOSE + 1:
-                project_keys(0)
-            if u == -LEAD_TRANSPOSE + 2:
-                project_keys(1)
             ut, ux, up, uq = u + LEAD_TRANSPOSE, u + LEAD_QUANTISE_X, u + LEAD_PROJECT, u + LEAD_QUANTISE_Q
             if exists(u):
-                for j in range(BANKS // 2):
-                    fill_bank(u, j)
-            if exists(ut):
+                fill_bank(u, 0)
+                if paired(u):
+                    fill_paired(u)
+                    part(u)
+                else:
+                    fill_bank(u, 2)
+            if exists(ut) and exists(u):
                 x_grouped[ut] = features_to_partitions(x_raw[ut], nc.scalar.copy, "xt", 2)
             if exists(up):
                 q_planar[up] = new_planar()
-            for j in range(BANKS // 2):
+            for i in range(2):
                 if exists(u):
-                    take_max(u, j)
-                    fill_bank(u, j + BANKS // 2)
+                    if i == 0 or not paired(u):
+                        take_max(u, 2 * i)
+                    fill_bank(u, 2 * i + 1)
                 if exists(up):
-                    project_pair(wq_mx, x_mx[up], bq_f, q_planar[up], j, (scalar_add_bias, scalar_add_bias), "proj", 2)
+                    project_pair(wq_mx, x_mx[up], bq_bf, q_planar[up], i, (scalar_add_bias, scalar_add_bias), "proj", 2)
             if exists(ux):
                 x_mx[ux] = mx_tiles(stage, "x", ROWS)
                 quantise(x_grouped[ux], x_mx[ux])
@@ -220,10 +284,27 @@ def tile_attention_pa_t_kernel(tc, query_states, key_states, Wq, bq, Wk, bk, log
             if exists(up):
                 q_grouped[up] = new_grouped_out()
                 regroup_queries(q_planar[up], q_grouped[up])
+            if paired(u):
+                add_parts(u)
+            if exists(ut) and not exists(u):
+                x_grouped[ut] = features_to_partitions(x_raw[ut], nc.scalar.copy, "xt", 2)
+            if u == -LEAD_TRANSPOSE:
+                ks_grouped.append(spread(ks_raw[1], nc.vector.tensor_copy))
+            if u == -LEAD_QUANTISE_X:
+                quantise(ks_grouped[1], half_of(ks_mx, 1))
+            if u == -LEAD_PROJECT:
+                project_keys(1)
+            if u == 0:
+                for i in range(3):
+                    quantise(split_grouped[i], split_mx[i])
             if exists(u):
-                for j in range(BANKS // 2, BANKS):
-                    take_max(u, j)
+                take_max(u, 1)
+                take_max(u, 3)
+            if paired(u - 1):
+                take_paired_max(u - 1)
 
+        gain = const.tile([P, 1], F32, name="gain")
+        nc.scalar.activation(out=gain, in_=ls_bf, func=ACT.Exp)
         sums = psum.tile([P, BQ * BK], F32, name="sums", tag="r", bufs=4)
         nc.tensor.matmul(out=sums, lhsT=ones, rhs=row_max.rearrange("p a b -> p (a b)"), start=True, stop=False)
         nc.tensor.matmul(out=sums, lhsT=ones, rhs=col_max.rearrange("p a b -> p (a b)"), start=False, stop=True)

@@ -26,9 +26,10 @@ SPLIT = BK * L // 2
 
 FIRST_PAIRED = 2
 
-LEAD_TRANSPOSE = 4
-LEAD_QUANTISE_X = 3
-LEAD_PROJECT = 2
+LEAD_TRANSPOSE = 5
+LEAD_QUANTISE_X = 4
+LEAD_PROJECT = 3
+LEAD_REGROUP = 2
 LEAD_QUANTISE_Q = 1
 
 FLOPS = 2 * D * D * (BQ + BK) * L + 2 * (BQ * L) * (BK * L) * D
@@ -75,6 +76,10 @@ def tile_attention_pa_t_kernel(tc, query_states, key_states, Wq, bq, Wk, bk, log
         make_identity(nc, ident)
         ones = const.tile([P, P], F32, name="ones")
         nc.gpsimd.memset(ones, 1.0)
+        first_exp = const.tile([P, 1], F32, name="first_exp")
+        nc.scalar.activation(out=first_exp, in_=ones[:, 0:1], func=ACT.Exp)
+        bq_f = const.tile([P, PACK], F32, name="bq_f")
+        nc.gpsimd.tensor_copy(out=bq_f, in_=bq_bf)
 
         def mx_tiles(pool, name, columns):
             codes = pool.tile([P, columns], U32, name=name + "_codes", tag=name + "_codes", align_bytes=64)
@@ -256,7 +261,8 @@ def tile_attention_pa_t_kernel(tc, query_states, key_states, Wq, bq, Wk, bk, log
             )
 
         for u in range(-LEAD_TRANSPOSE, N_UNITS):
-            ut, ux, up, uq = u + LEAD_TRANSPOSE, u + LEAD_QUANTISE_X, u + LEAD_PROJECT, u + LEAD_QUANTISE_Q
+            ut, ux, up = u + LEAD_TRANSPOSE, u + LEAD_QUANTISE_X, u + LEAD_PROJECT
+            ur, uq = u + LEAD_REGROUP, u + LEAD_QUANTISE_Q
             if exists(u):
                 fill_bank(u, 0)
                 if paired(u):
@@ -274,16 +280,16 @@ def tile_attention_pa_t_kernel(tc, query_states, key_states, Wq, bq, Wk, bk, log
                         take_max(u, 2 * i)
                     fill_bank(u, 2 * i + 1)
                 if exists(up):
-                    project_pair(wq_mx, x_mx[up], bq_bf, q_planar[up], i, (scalar_add_bias, scalar_add_bias), "proj", 2)
+                    project_pair(wq_mx, x_mx[up], bq_f, q_planar[up], i, (scalar_add_bias, scalar_add_bias), "proj", 2)
             if exists(ux):
                 x_mx[ux] = mx_tiles(stage, "x", ROWS)
                 quantise(x_grouped[ux], x_mx[ux])
             if exists(uq):
                 q_mx[uq] = mx_tiles(stage, "q", ROWS)
                 quantise(q_grouped[uq], q_mx[uq])
-            if exists(up):
-                q_grouped[up] = new_grouped_out()
-                regroup_queries(q_planar[up], q_grouped[up])
+            if exists(ur):
+                q_grouped[ur] = new_grouped_out()
+                regroup_queries(q_planar[ur], q_grouped[ur])
             if paired(u):
                 add_parts(u)
             if exists(ut) and not exists(u):

from contextlib import ExitStack

import concourse.mybir as mybir
from concourse.masks import make_identity

F32 = mybir.dt.float32
BF16 = mybir.dt.bfloat16
U32 = mybir.dt.uint32
U8 = mybir.dt.uint8
FP8X4 = mybir.dt.float8_e4m3fn_x4
ALU = mybir.AluOpType
ACT = mybir.ActivationFunctionType
AXIS_X = mybir.AxisListType.X

P = 128
PACK = 4
BQ, BK, L, D = 64, 4, 128, 512
WORDS = D // 2
UNIT = 2
ROWS = UNIT * L
N_UNITS = BQ // UNIT
HALVES = D // ROWS

POOL_ROWS = 192
SPLIT = BK * L // 2

FIRST_PAIRED = 2

LEAD_TRANSPOSE = 5
LEAD_QUANTISE_X = 4
LEAD_PROJECT = 3
LEAD_REGROUP = 2
LEAD_QUANTISE_Q = 1

FLOPS = 2 * D * D * (BQ + BK) * L + 2 * (BQ * L) * (BK * L) * D


def tile_attention_pa_t_kernel(tc, query_states, key_states, Wq, bq, Wk, bk, logit_scale, out):
    nc = tc.nc
    with ExitStack() as stack:
        const = stack.enter_context(tc.tile_pool(name="const", bufs=1))
        xpool = stack.enter_context(tc.tile_pool(name="xpool", bufs=N_UNITS))
        stage = stack.enter_context(tc.tile_pool(name="stage", bufs=4))
        psum = stack.enter_context(tc.psum_pool(name="psum", bufs=2))

        def load(pool, name, rows):
            raw = pool.tile([P, UNIT * D], BF16, name=name, tag=name)
            nc.sync.dma_start(out=raw.rearrange("p (s d) -> p s d", s=UNIT), in_=rows)
            return raw

        wk_rows = Wk.rearrange("(m t) d -> m t d", t=PACK)
        wq_rows = Wq.rearrange("(m t) d -> m t d", t=PACK)
        ks_rows = key_states.rearrange("s l d -> l s d")
        xs_rows = query_states.rearrange("s l d -> l s d")
        def load_half(name, rows, h):
            return load(const, "%s_raw%d" % (name, h), rows[:, h * UNIT : (h + 1) * UNIT, :])

        def load_x(u):
            return load(xpool, "x_raw", xs_rows[:, u * UNIT : (u + 1) * UNIT, :])

        wk_raw = [load_half("wk", wk_rows, h) for h in range(HALVES)]
        ks_raw = [load_half("ks", ks_rows, 0)]
        wq_raw = [load_half("wq", wq_rows, h) for h in range(HALVES)]
        x_raw = [load_x(0)]
        ks_raw.append(load_half("ks", ks_rows, 1))
        x_raw.extend([load_x(u) for u in range(1, N_UNITS)])

        bk_bf = const.tile([P, PACK], BF16, name="bk_bf")
        bq_bf = const.tile([P, PACK], BF16, name="bq_bf")
        ls_bf = const.tile([P, 1], BF16, name="ls_bf")
        nc.scalar.dma_start(out=bk_bf, in_=bk.rearrange("(p t) -> p t", t=PACK))
        nc.scalar.dma_start(out=bq_bf, in_=bq.rearrange("(p t) -> p t", t=PACK))
        nc.scalar.dma_start(out=ls_bf, in_=logit_scale.partition_broadcast(P))

        ident = const.tile([P, P], F32, name="ident")
        make_identity(nc, ident)
        ones = const.tile([P, P], F32, name="ones")
        nc.gpsimd.memset(ones, 1.0)
        first_exp = const.tile([P, 1], F32, name="first_exp")
        nc.scalar.activation(out=first_exp, in_=ones[:, 0:1], func=ACT.Exp)
        bq_f = const.tile([P, PACK], F32, name="bq_f")
        nc.gpsimd.tensor_copy(out=bq_f, in_=bq_bf)

        def mx_tiles(pool, name, columns):
            codes = pool.tile([P, columns], U32, name=name + "_codes", tag=name + "_codes", align_bytes=64)
            scales = pool.tile([P, columns], U8, name=name + "_scales", tag=name + "_scales", align_bytes=64)
            return codes, scales

        def columns_of(operand, first, count):
            return operand[0][:, first : first + count], operand[1][:, first : first + count]

        def quantise(grouped, operand):
            nc.vector.quantize_mx(out=operand[0].bitcast(FP8X4), scales=operand[1], in_=grouped)

        def multiply(acc, stationary, moving, start=True, stop=True):
            nc.tensor.matmul_mx(
                out=acc,
                lhsT=stationary[0].bitcast(FP8X4),
                lhsT_scale=stationary[1],
                rhs=moving[0].bitcast(FP8X4),
                rhs_scale=moving[1],
                start=start,
                stop=stop,
            )

        def features_to_partitions(raw, copy, tag, bufs):
            raw_words = raw.bitcast(F32)
            bank = psum.tile([P, UNIT, 2, P], F32, name="xt", tag=tag, bufs=bufs)
            for s in range(UNIT):
                for u in range(2):
                    first = s * WORDS + u * P
                    nc.tensor.transpose(bank[:, s, u, :], raw_words[:, first : first + P], ident)
            grouped = stage.tile([P, ROWS * PACK], BF16, name="grouped_in", tag="grouped_in", bufs=6, align_bytes=64)
            copy(
                out=grouped.bitcast(F32).rearrange("p (s r u) -> p s r u", s=UNIT, u=2),
                in_=bank.rearrange("p s u r -> p s r u"),
            )
            return grouped

        def scalar_add_bias(dst, acc, bias):
            nc.scalar.activation(out=dst, in_=acc, func=ACT.Identity, bias=bias, scale=1.0)

        def project_pair(weights, rows, bias, planar, pair, add_bias, tag, bufs):
            bank = psum.tile([P, 2, ROWS], F32, name="proj", tag=tag, bufs=bufs)
            for i in range(2):
                multiply(bank[:, i, :], columns_of(weights, (2 * pair + i) * P, P), rows)
            for i in range(2):
                t = 2 * pair + i
                add_bias[i](planar[:, t, :], bank[:, i, :], bias[:, t : t + 1])

        def new_planar():
            return stage.tile([P, PACK, ROWS], BF16, name="planar", tag="planar")

        def new_grouped_out():
            return stage.tile([P, ROWS * PACK], BF16, name="grouped_out", tag="grouped_out", bufs=1, align_bytes=64)

        wk_mx = mx_tiles(const, "wk", D)
        ks_mx = mx_tiles(const, "ks", D)
        wq_mx = mx_tiles(const, "wq", D)
        k_mx = mx_tiles(const, "k", D)
        split_mx = [mx_tiles(const, "split%d" % i, SPLIT) for i in range(3)]
        split_grouped = []
        for i in range(3):
            half = const.tile([P, SPLIT * PACK], BF16, name="split_grouped%d" % i, align_bytes=64)
            split_grouped.append(half)
        def spread(raw, copy):
            return features_to_partitions(raw, copy, "r", 4)

        def half_of(operand, h):
            return columns_of(operand, h * ROWS, ROWS)

        def project_keys(h):
            grouped = stage.tile([P, ROWS * PACK], BF16, name="grouped_k", tag="grouped_k", bufs=2, align_bytes=64)
            for s in range(UNIT):
                bank = psum.tile([P, PACK, L], F32, name="keys", tag="r", bufs=4)
                for t in range(PACK):
                    multiply(bank[:, t, :], columns_of(wk_mx, t * P, P), columns_of(ks_mx, (h * UNIT + s) * L, L))
                nc.vector.tensor_tensor(
                    out=grouped[:, s * L * PACK : (s + 1) * L * PACK].rearrange("p (m t) -> p m t", t=PACK),
                    in0=bank.rearrange("p t m -> p m t"),
                    in1=bk_bf.unsqueeze(1).to_broadcast([P, L, PACK]),
                    op=ALU.add,
                )
            quantise(grouped, half_of(k_mx, h))
            by_half = grouped.rearrange("p (b c v) -> p b c v", b=UNIT, c=2)
            for i in range(3):
                nc.gpsimd.tensor_scalar(
                    out=split_grouped[i][:, h * ROWS * 2 : (h + 1) * ROWS * 2].rearrange("p (b v) -> p b v", b=UNIT),
                    in0=by_half[:, :, min(i, 1), :],
                    scalar1=-1.0 if i == 2 else 1.0,
                    scalar2=0.0,
                    op0=ALU.mult,
                    op1=ALU.add,
                )

        wk_grouped = [spread(wk_raw[0], nc.vector.tensor_copy), spread(wk_raw[1], nc.scalar.copy)]
        ks_grouped = [spread(ks_raw[0], nc.vector.tensor_copy)]
        for h in range(HALVES):
            quantise(wk_grouped[h], half_of(wk_mx, h))
        quantise(ks_grouped[0], half_of(ks_mx, 0))
        wq_grouped = [spread(wq_raw[0], nc.scalar.copy), spread(wq_raw[1], nc.scalar.copy)]
        project_keys(0)
        for h in range(HALVES):
            quantise(wq_grouped[h], half_of(wq_mx, h))

        row_max = const.tile([P, BQ, BK], F32, name="row_max")
        col_max = const.tile([P, BQ, BK], F32, name="col_max")
        x_grouped = {}
        x_mx = {}
        q_planar = {}
        q_grouped = {}
        q_mx = {}
        scores = {}
        BANKS = 2 * UNIT

        def fill_bank(u, j):
            bank = psum.tile([P, 2, 2, L], F32, name="scores", tag="r", bufs=4)
            if j % 2 == 0:
                multiply(bank.rearrange("p c d m -> p (c d m)"), columns_of(q_mx[u], (j // 2) * L, L), k_mx)
            else:
                for i in range(2):
                    multiply(bank[:, i, :, :].rearrange("p a l -> p (a l)"), columns_of(k_mx, (j - 1 + i) * L, L), q_mx[u])
            scores[j] = bank

        def take_max(u, j):
            if j % 2 == 0:
                maxima = row_max[:, u * UNIT + j // 2, :].rearrange("p (c d) -> p c d", c=2)
            else:
                maxima = col_max[:, u * UNIT : (u + 1) * UNIT, j - 1 : j + 1].rearrange("p a b -> p b a")
            nc.vector.tensor_reduce(out=maxima, in_=scores[j], axis=AXIS_X, op=ALU.max)

        def regroup_queries(planar, grouped):
            nc.gpsimd.tensor_scalar(
                out=grouped[:, : POOL_ROWS * PACK].rearrange("p (r t) -> p r t", t=PACK),
                in0=planar[:, :, :POOL_ROWS].rearrange("p t r -> p r t"),
                scalar1=1.0,
                scalar2=0.0,
                op0=ALU.mult,
                op1=ALU.add,
            )
            nc.scalar.copy(
                out=grouped[:, POOL_ROWS * PACK :].rearrange("p (c i t) -> p c t i", i=4, t=PACK),
                in_=planar[:, :, POOL_ROWS:].rearrange("p t (c i) -> p c t i", i=4),
            )

        def exists(u):
            return 0 <= u < N_UNITS

        paired_sums = {}
        parts_of = {}

        def paired(u):
            return FIRST_PAIRED <= u < N_UNITS - 2

        def fill_paired(u):
            q_sample = columns_of(q_mx[u], L, L)
            bank = psum.tile([P, 2, SPLIT], F32, name="scores", tag="r", bufs=4)
            multiply(bank[:, 0, :], q_sample, split_mx[0], stop=False)
            multiply(bank[:, 0, :], q_sample, split_mx[2], start=False)
            multiply(bank[:, 1, :], q_sample, split_mx[1])
            scores[2] = bank

        def part(u):
            parts = stage.tile([P, 2, SPLIT], F32, name="parts", tag="parts")
            nc.scalar.activation(out=parts[:, 0, :], in_=scores[2][:, 0, :], func=ACT.Relu)
            nc.scalar.copy(out=parts[:, 1, :], in_=scores[2][:, 1, :])
            parts_of[u] = parts

        def add_parts(u):
            parts = parts_of[u]
            paired_sum = stage.tile([P, SPLIT], F32, name="paired_sum", tag="paired_sum")
            nc.gpsimd.tensor_tensor(out=paired_sum, in0=parts[:, 0, :], in1=parts[:, 1, :], op=ALU.add)
            paired_sums[u] = paired_sum

        def take_paired_max(u):
            nc.vector.tensor_reduce(
                out=row_max[:, u * UNIT + 1, :],
                in_=paired_sums[u].rearrange("p (b m) -> p b m", b=BK),
                axis=AXIS_X,
                op=ALU.max,
            )

        for u in range(-LEAD_TRANSPOSE, N_UNITS):
            ut, ux, up = u + LEAD_TRANSPOSE, u + LEAD_QUANTISE_X, u + LEAD_PROJECT
            ur, uq = u + LEAD_REGROUP, u + LEAD_QUANTISE_Q
            if exists(u):
                fill_bank(u, 0)
                if paired(u):
                    fill_paired(u)
                    part(u)
                else:
                    fill_bank(u, 2)
            if exists(ut) and exists(u):
                x_grouped[ut] = features_to_partitions(x_raw[ut], nc.scalar.copy, "xt", 2)
            if exists(up):
                q_planar[up] = new_planar()
            for i in range(2):
                if exists(u):
                    if i == 0 or not paired(u):
                        take_max(u, 2 * i)
                    fill_bank(u, 2 * i + 1)
                if exists(up):
                    project_pair(wq_mx, x_mx[up], bq_f, q_planar[up], i, (scalar_add_bias, scalar_add_bias), "proj", 2)
            if exists(ux):
                x_mx[ux] = mx_tiles(stage, "x", ROWS)
                quantise(x_grouped[ux], x_mx[ux])
            if exists(uq):
                q_mx[uq] = mx_tiles(stage, "q", ROWS)
                quantise(q_grouped[uq], q_mx[uq])
            if exists(ur):
                q_grouped[ur] = new_grouped_out()
                regroup_queries(q_planar[ur], q_grouped[ur])
            if paired(u):
                add_parts(u)
            if exists(ut) and not exists(u):
                x_grouped[ut] = features_to_partitions(x_raw[ut], nc.scalar.copy, "xt", 2)
            if u == -LEAD_TRANSPOSE:
                ks_grouped.append(spread(ks_raw[1], nc.vector.tensor_copy))
            if u == -LEAD_QUANTISE_X:
                quantise(ks_grouped[1], half_of(ks_mx, 1))
            if u == -LEAD_PROJECT:
                project_keys(1)
            if u == 0:
                for i in range(3):
                    quantise(split_grouped[i], split_mx[i])
            if exists(u):
                take_max(u, 1)
                take_max(u, 3)
            if paired(u - 1):
                take_paired_max(u - 1)

        gain = const.tile([P, 1], F32, name="gain")
        nc.scalar.activation(out=gain, in_=ls_bf, func=ACT.Exp)
        sums = psum.tile([P, BQ * BK], F32, name="sums", tag="r", bufs=4)
        nc.tensor.matmul(out=sums, lhsT=ones, rhs=row_max.rearrange("p a b -> p (a b)"), start=True, stop=False)
        nc.tensor.matmul(out=sums, lhsT=ones, rhs=col_max.rearrange("p a b -> p (a b)"), start=False, stop=True)
        result = const.tile([P, BQ * BK], F32, name="result")
        nc.vector.tensor_scalar(
            out=result, in0=sums, scalar1=gain[:, 0:1], scalar2=1.0 / (2 * L), op0=ALU.mult, op1=ALU.mult
        )
        nc.sync.dma_start(out=out.rearrange("(o a) b -> o (a b)", o=1), in_=result[0:1, :])
